import numpy as np
import ml_dtypes

BF16 = ml_dtypes.bfloat16


def bf(x):
    return np.asarray(x, np.float32).astype(BF16)


def f32(x):
    return np.asarray(x, np.float32)


def f64(x):
    return np.asarray(x).astype(np.float64)


def striped(idx):
    return np.tile(idx.reshape(-1, 16).T, (8, 1))


H, D, C, P, N, S = 2, 128, 256, 256, 512, 1024


def setup_inputs():
    return {"q": bf(np.random.standard_normal((C, N))), "k": bf(np.random.standard_normal((C, N))), "v": bf(4.0 * np.random.standard_normal((N, C))), "k_past": bf(np.random.standard_normal((C, P))), "v_past": bf(4.0 * np.random.standard_normal((P, C))), "base": f32(0.25 * np.random.standard_normal((C, S))), "offs": striped(np.random.permutation(S)[:N])}


def reference(q, k, v, k_past, v_past, base, offs):
    idx = offs[:16].T.reshape(-1)
    keys = np.concatenate([f64(k_past), f64(k)], axis=1).reshape(H, D, P + N)
    vals = np.concatenate([f64(v_past), f64(v)], axis=0).reshape(P + N, H, D)
    qs = f64(q).reshape(H, D, N)
    e = np.exp(np.einsum('hdt,hdn->htn', keys, qs) / np.sqrt(D))
    num = np.einsum('thd,htn->hdn', vals, e)
    r = 1.0 / e.sum(axis=1)
    out = f64(base).copy()
    out[:, idx] = (num * r[:, None, :]).reshape(C, N)
    return out

@@ -1,0 +1,67 @@
+import math
+
+import concourse.mybir as mybir
+
+HEADS = 2
+FEATURES = 128
+PAST = 256
+NEW = 512
+SLOTS = 1024
+TOKENS = PAST + NEW
+BLOCKS = TOKENS // 128
+
+BF16 = mybir.dt.bfloat16
+F32 = mybir.dt.float32
+U16 = mybir.dt.uint16
+
+FLOPS = 2 * 2 * HEADS * FEATURES * TOKENS * NEW
+
+
+def tile_conditionalmodel2_kernel(tc, q, k, v, k_past, v_past, base, offs, out):
+    nc = tc.nc
+    exp = mybir.ActivationFunctionType.Exp
+    mult = mybir.AluOpType.mult
+
+    with (
+        tc.tile_pool(name="held", bufs=1) as held,
+        tc.tile_pool(name="weights", bufs=4) as weights,
+        tc.tile_pool(name="inverse", bufs=2) as inverse,
+        tc.psum_pool(name="score_banks", bufs=3) as score_banks,
+        tc.psum_pool(name="sum_banks", bufs=2) as sum_banks,
+    ):
+        keys = [held.tile([FEATURES, TOKENS], BF16, name=f"keys{h}") for h in range(HEADS)]
+        queries = [held.tile([FEATURES, NEW], BF16, name=f"queries{h}") for h in range(HEADS)]
+        windows = [held.tile([FEATURES, SLOTS], F32, name=f"window{h}") for h in range(HEADS)]
+        vals = held.tile([128, BLOCKS, HEADS * FEATURES], BF16, name="vals")
+        offsets = held.tile([128, NEW // 16], U16, name="offsets")
+        for h in range(HEADS):
+            rows = slice(h * FEATURES, (h + 1) * FEATURES)
+            nc.sync.dma_start(keys[h][:, 0:PAST], k_past[rows, :])
+            nc.scalar.dma_start(queries[h][:], q[rows, :])
+            nc.sync.dma_start(keys[h][:, PAST:TOKENS], k[rows, :])
+        nc.scalar.dma_start(vals[:, 0 : PAST // 128, :], v_past.rearrange("(b p) c -> p b c", p=128))
+        nc.scalar.dma_start(vals[:, PAST // 128 : BLOCKS, :], v.rearrange("(b p) c -> p b c", p=128))
+        nc.sync.dma_start(offsets[:], offs)
+        for h in range(HEADS):
+            nc.gpsimd.dma_start(windows[h][:], base[h * FEATURES : (h + 1) * FEATURES, :])
+
+        ones = held.tile([128, FEATURES], BF16, name="ones")
+        nc.vector.memset(ones[:], 1.0)
+
+        for h in range(HEADS):
+            num = sum_banks.tile([FEATURES, NEW], F32, name="num")
+            total = sum_banks.tile([FEATURES, NEW], F32, name="total")
+            for b in range(BLOCKS):
+                first, last = b == 0, b == BLOCKS - 1
+                scores = score_banks.tile([128, NEW], F32, name="scores")
+                nc.tensor.matmul(scores[:], keys[h][:, b * 128 : (b + 1) * 128], queries[h][:], start=True, stop=True)
+                e = weights.tile([128, NEW], BF16, name="e")
+                nc.scalar.activation(e[:], scores[:], exp, scale=1.0 / math.sqrt(FEATURES))
+                nc.tensor.matmul(num[:], vals[:, b, h * FEATURES : (h + 1) * FEATURES], e[:], start=first, stop=last)
+                nc.tensor.matmul(total[:], ones[:], e[:], start=first, stop=last)
+            r = inverse.tile([FEATURES, NEW], F32, name="r")
+            nc.vector.reciprocal(r[:], total[:])
+            num_sb = inverse.tile([FEATURES, NEW], F32, name="num_sb")
+            nc.scalar.copy(num_sb[:], num[:])
+            nc.vector.tensor_tensor(windows[h][:].indirect(offsets[:]), num_sb[:], r[:], mult)
+            nc.sync.dma_start(out[h * FEATURES : (h + 1) * FEATURES, :], windows[h][:])

@@ -1,6 +1,7 @@
 import math
 
 import concourse.mybir as mybir
+from concourse.masks import make_identity
 
 HEADS = 2
 FEATURES = 128
@@ -9,6 +10,9 @@ NEW = 512
 SLOTS = 1024
 TOKENS = PAST + NEW
 BLOCKS = TOKENS // 128
+PIECE = 512
+PIECES = NEW // PIECE
+SUBS = PIECE // 128
 
 BF16 = mybir.dt.bfloat16
 F32 = mybir.dt.float32
@@ -25,9 +29,11 @@ def tile_conditionalmodel2_kernel(tc, q, k, v, k_past, v_past, base, offs, out):
     with (
         tc.tile_pool(name="held", bufs=1) as held,
         tc.tile_pool(name="weights", bufs=4) as weights,
-        tc.tile_pool(name="inverse", bufs=2) as inverse,
+        tc.tile_pool(name="factors", bufs=2) as factors,
         tc.psum_pool(name="score_banks", bufs=3) as score_banks,
-        tc.psum_pool(name="sum_banks", bufs=2) as sum_banks,
+        tc.psum_pool(name="num_banks", bufs=2) as num_banks,
+        tc.psum_pool(name="total_banks", bufs=2) as total_banks,
+        tc.psum_pool(name="spread_banks", bufs=1) as spread_banks,
     ):
         keys = [held.tile([FEATURES, TOKENS], BF16, name=f"keys{h}") for h in range(HEADS)]
         queries = [held.tile([FEATURES, NEW], BF16, name=f"queries{h}") for h in range(HEADS)]
@@ -43,25 +49,54 @@ def tile_conditionalmodel2_kernel(tc, q, k, v, k_past, v_past, base, offs, out):
         nc.scalar.dma_start(vals[:, PAST // 128 : BLOCKS, :], v.rearrange("(b p) c -> p b c", p=128))
         nc.sync.dma_start(offsets[:], offs)
         for h in range(HEADS):
-            nc.gpsimd.dma_start(windows[h][:], base[h * FEATURES : (h + 1) * FEATURES, :])
+            nc.sync.dma_start(windows[h][:], base[h * FEATURES : (h + 1) * FEATURES, :])
 
-        ones = held.tile([128, FEATURES], BF16, name="ones")
-        nc.vector.memset(ones[:], 1.0)
+        picks = held.tile([128, SUBS, SUBS], BF16, name="picks")
+        nc.vector.memset(picks[:], 0.0)
+        for s in range(SUBS):
+            nc.vector.memset(picks[:, s, s : s + 1], 1.0)
+        identity = held.tile([128, 128], F32, name="identity")
+        make_identity(nc, identity[:])
 
         for h in range(HEADS):
-            num = sum_banks.tile([FEATURES, NEW], F32, name="num")
-            total = sum_banks.tile([FEATURES, NEW], F32, name="total")
-            for b in range(BLOCKS):
-                first, last = b == 0, b == BLOCKS - 1
-                scores = score_banks.tile([128, NEW], F32, name="scores")
-                nc.tensor.matmul(scores[:], keys[h][:, b * 128 : (b + 1) * 128], queries[h][:], start=True, stop=True)
-                e = weights.tile([128, NEW], BF16, name="e")
-                nc.scalar.activation(e[:], scores[:], exp, scale=1.0 / math.sqrt(FEATURES))
-                nc.tensor.matmul(num[:], vals[:, b, h * FEATURES : (h + 1) * FEATURES], e[:], start=first, stop=last)
-                nc.tensor.matmul(total[:], ones[:], e[:], start=first, stop=last)
-            r = inverse.tile([FEATURES, NEW], F32, name="r")
-            nc.vector.reciprocal(r[:], total[:])
-            num_sb = inverse.tile([FEATURES, NEW], F32, name="num_sb")
-            nc.scalar.copy(num_sb[:], num[:])
-            nc.vector.tensor_tensor(windows[h][:].indirect(offsets[:]), num_sb[:], r[:], mult)
+            for piece in range(PIECES):
+                columns = slice(piece * PIECE, (piece + 1) * PIECE)
+                num = num_banks.tile([FEATURES, PIECE], F32, name="num")
+                totals = total_banks.tile([128, SUBS], F32, name="totals")
+                for b in range(BLOCKS):
+                    first, last = b == 0, b == BLOCKS - 1
+                    scores = score_banks.tile([128, PIECE], F32, name="scores")
+                    nc.tensor.matmul(
+                        scores[:], keys[h][:, b * 128 : (b + 1) * 128], queries[h][:, columns], start=True, stop=True
+                    )
+                    e = weights.tile([128, PIECE], BF16, name="e")
+                    nc.scalar.activation(e[:], scores[:], exp, scale=1.0 / math.sqrt(FEATURES))
+                    nc.tensor.matmul(
+                        num[:], vals[:, b, h * FEATURES : (h + 1) * FEATURES], e[:], start=first, stop=last
+                    )
+                    for s in range(SUBS):
+                        nc.tensor.matmul(
+                            totals[:],
+                            e[:, s * 128 : (s + 1) * 128],
+                            picks[:, s, :],
+                            start=first and s == 0,
+                            stop=last and s == SUBS - 1,
+                        )
+                r_column = factors.tile([128, SUBS], F32, name="r_column")
+                nc.vector.reciprocal(r_column[:], totals[:])
+                spread = spread_banks.tile([FEATURES, PIECE], F32, name="spread")
+                for s in range(SUBS):
+                    nc.tensor.transpose(
+                        spread[:, s * 128 : (s + 1) * 128], r_column[:, s : s + 1].to_broadcast([128, 128]), identity[:]
+                    )
+                r = factors.tile([FEATURES, PIECE], F32, name="r")
+                nc.vector.tensor_copy(r[:], spread[:])
+                num_sb = factors.tile([FEATURES, PIECE], F32, name="num_sb")
+                nc.scalar.copy(num_sb[:], num[:])
+                nc.vector.tensor_tensor(
+                    windows[h][:].indirect(offsets[:, piece * (PIECE // 16) : (piece + 1) * (PIECE // 16)]),
+                    num_sb[:],
+                    r[:],
+                    mult,
+                )
             nc.sync.dma_start(out[h * FEATURES : (h + 1) * FEATURES, :], windows[h][:])

@@ -10,9 +10,10 @@ NEW = 512
 SLOTS = 1024
 TOKENS = PAST + NEW
 BLOCKS = TOKENS // 128
-PIECE = 512
+PIECE = 256
 PIECES = NEW // PIECE
 SUBS = PIECE // 128
+WARM_UP = 4
 
 BF16 = mybir.dt.bfloat16
 F32 = mybir.dt.float32
@@ -28,7 +29,7 @@ def tile_conditionalmodel2_kernel(tc, q, k, v, k_past, v_past, base, offs, out):
 
     with (
         tc.tile_pool(name="held", bufs=1) as held,
-        tc.tile_pool(name="weights", bufs=4) as weights,
+        tc.tile_pool(name="weights", bufs=6) as weights,
         tc.tile_pool(name="factors", bufs=2) as factors,
         tc.psum_pool(name="score_banks", bufs=3) as score_banks,
         tc.psum_pool(name="num_banks", bufs=2) as num_banks,
@@ -40,16 +41,24 @@ def tile_conditionalmodel2_kernel(tc, q, k, v, k_past, v_past, base, offs, out):
         windows = [held.tile([FEATURES, SLOTS], F32, name=f"window{h}") for h in range(HEADS)]
         vals = held.tile([128, BLOCKS, HEADS * FEATURES], BF16, name="vals")
         offsets = held.tile([128, NEW // 16], U16, name="offsets")
-        for h in range(HEADS):
-            rows = slice(h * FEATURES, (h + 1) * FEATURES)
-            nc.sync.dma_start(keys[h][:, 0:PAST], k_past[rows, :])
-            nc.scalar.dma_start(queries[h][:], q[rows, :])
-            nc.sync.dma_start(keys[h][:, PAST:TOKENS], k[rows, :])
+        head_rows = [slice(h * FEATURES, (h + 1) * FEATURES) for h in range(HEADS)]
+        nc.sync.dma_start(keys[0][:, 0:PAST], k_past[head_rows[0], :])
+        nc.scalar.dma_start(queries[0][:], q[head_rows[0], :])
         nc.scalar.dma_start(vals[:, 0 : PAST // 128, :], v_past.rearrange("(b p) c -> p b c", p=128))
+        nc.sync.dma_start(keys[0][:, PAST:TOKENS], k[head_rows[0], :])
         nc.scalar.dma_start(vals[:, PAST // 128 : BLOCKS, :], v.rearrange("(b p) c -> p b c", p=128))
+        nc.sync.dma_start(keys[1][:, 0:PAST], k_past[head_rows[1], :])
+        nc.scalar.dma_start(queries[1][:], q[head_rows[1], :])
+        nc.sync.dma_start(keys[1][:, PAST:TOKENS], k[head_rows[1], :])
         nc.sync.dma_start(offsets[:], offs)
-        for h in range(HEADS):
-            nc.sync.dma_start(windows[h][:], base[h * FEATURES : (h + 1) * FEATURES, :])
+        nc.sync.dma_start(windows[0][:], base[head_rows[0], :])
+        nc.scalar.dma_start(windows[1][:], base[head_rows[1], :])
+
+        zeros = held.tile([128, 512], BF16, name="zeros")
+        nc.vector.memset(zeros[:], 0.0)
+        warm = spread_banks.tile([128, 512], F32, name="warm", tag="spread")
+        for repeat in range(WARM_UP):
+            nc.tensor.matmul(warm[:], zeros[:, 0:128], zeros[:], start=True, stop=True)
 
         picks = held.tile([128, SUBS, SUBS], BF16, name="picks")
         nc.vector.memset(picks[:], 0.0)
@@ -58,45 +67,72 @@ def tile_conditionalmodel2_kernel(tc, q, k, v, k_past, v_past, base, offs, out):
         identity = held.tile([128, 128], F32, name="identity")
         make_identity(nc, identity[:])
 
-        for h in range(HEADS):
-            for piece in range(PIECES):
-                columns = slice(piece * PIECE, (piece + 1) * PIECE)
-                num = num_banks.tile([FEATURES, PIECE], F32, name="num")
-                totals = total_banks.tile([128, SUBS], F32, name="totals")
-                for b in range(BLOCKS):
-                    first, last = b == 0, b == BLOCKS - 1
-                    scores = score_banks.tile([128, PIECE], F32, name="scores")
-                    nc.tensor.matmul(
-                        scores[:], keys[h][:, b * 128 : (b + 1) * 128], queries[h][:, columns], start=True, stop=True
-                    )
-                    e = weights.tile([128, PIECE], BF16, name="e")
-                    nc.scalar.activation(e[:], scores[:], exp, scale=1.0 / math.sqrt(FEATURES))
-                    nc.tensor.matmul(
-                        num[:], vals[:, b, h * FEATURES : (h + 1) * FEATURES], e[:], start=first, stop=last
-                    )
-                    for s in range(SUBS):
-                        nc.tensor.matmul(
-                            totals[:],
-                            e[:, s * 128 : (s + 1) * 128],
-                            picks[:, s, :],
-                            start=first and s == 0,
-                            stop=last and s == SUBS - 1,
-                        )
-                r_column = factors.tile([128, SUBS], F32, name="r_column")
-                nc.vector.reciprocal(r_column[:], totals[:])
-                spread = spread_banks.tile([FEATURES, PIECE], F32, name="spread")
-                for s in range(SUBS):
-                    nc.tensor.transpose(
-                        spread[:, s * 128 : (s + 1) * 128], r_column[:, s : s + 1].to_broadcast([128, 128]), identity[:]
-                    )
-                r = factors.tile([FEATURES, PIECE], F32, name="r")
-                nc.vector.tensor_copy(r[:], spread[:])
-                num_sb = factors.tile([FEATURES, PIECE], F32, name="num_sb")
-                nc.scalar.copy(num_sb[:], num[:])
-                nc.vector.tensor_tensor(
-                    windows[h][:].indirect(offsets[:, piece * (PIECE // 16) : (piece + 1) * (PIECE // 16)]),
-                    num_sb[:],
-                    r[:],
-                    mult,
+        work = [(h, piece) for h in range(HEADS) for piece in range(PIECES)]
+        nums, totals, r_columns, factor_pairs = {}, {}, {}, {}
+
+        def attend(c, b):
+            h, piece = work[c]
+            first, last = b == 0, b == BLOCKS - 1
+            if first:
+                nums[c] = num_banks.tile([FEATURES, PIECE], F32, name="num")
+                totals[c] = total_banks.tile([128, SUBS], F32, name="totals")
+            scores = score_banks.tile([128, PIECE], F32, name="scores")
+            nc.tensor.matmul(
+                scores[:],
+                keys[h][:, b * 128 : (b + 1) * 128],
+                queries[h][:, piece * PIECE : (piece + 1) * PIECE],
+                start=True,
+                stop=True,
+            )
+            e = weights.tile([128, PIECE], BF16, name="e")
+            nc.scalar.activation(e[:], scores[:], exp, scale=1.0 / math.sqrt(FEATURES))
+            nc.tensor.matmul(nums[c][:], vals[:, b, head_rows[h]], e[:], start=first, stop=last)
+            for s in range(SUBS):
+                nc.tensor.matmul(
+                    totals[c][:],
+                    e[:, s * 128 : (s + 1) * 128],
+                    picks[:, s, :],
+                    start=first and s == 0,
+                    stop=last and s == SUBS - 1,
                 )
-            nc.sync.dma_start(out[h * FEATURES : (h + 1) * FEATURES, :], windows[h][:])
+
+        def invert(c):
+            r_columns[c] = factors.tile([128, SUBS], F32, name="r_column")
+            nc.vector.reciprocal(r_columns[c][:], totals[c][:])
+
+        def spread(c):
+            r_rows = spread_banks.tile([FEATURES, PIECE], F32, name="r_rows", tag="spread")
+            for s in range(SUBS):
+                nc.tensor.transpose(
+                    r_rows[:, s * 128 : (s + 1) * 128], r_columns[c][:, s : s + 1].to_broadcast([128, 128]), identity[:]
+                )
+            num_sb = factors.tile([FEATURES, PIECE], F32, name="num_sb")
+            nc.scalar.copy(num_sb[:], nums[c][:])
+            r = factors.tile([FEATURES, PIECE], F32, name="r")
+            nc.scalar.copy(r[:], r_rows[:])
+            factor_pairs[c] = (num_sb, r)
+
+        def place(c):
+            h, piece = work[c]
+            num_sb, r = factor_pairs[c]
+            nc.vector.tensor_tensor(
+                windows[h][:].indirect(offsets[:, piece * (PIECE // 16) : (piece + 1) * (PIECE // 16)]),
+                num_sb[:],
+                r[:],
+                mult,
+            )
+            if piece == PIECES - 1:
+                half = SLOTS // 2
+                nc.sync.dma_start(out[head_rows[h], 0:half], windows[h][:, 0:half])
+                nc.scalar.dma_start(out[head_rows[h], half:SLOTS], windows[h][:, half:SLOTS])
+
+        for c in range(len(work)):
+            for b in range(BLOCKS):
+                attend(c, b)
+                if b == 1 and c > 0:
+                    spread(c - 1)
+            invert(c)
+            if c > 0:
+                place(c - 1)
+        spread(len(work) - 1)
+        place(len(work) - 1)

@@ -10,10 +10,10 @@ NEW = 512
 SLOTS = 1024
 TOKENS = PAST + NEW
 BLOCKS = TOKENS // 128
+SUBS = NEW // 128
 PIECE = 256
 PIECES = NEW // PIECE
-SUBS = PIECE // 128
-WARM_UP = 4
+WARM_UP = 3
 
 BF16 = mybir.dt.bfloat16
 F32 = mybir.dt.float32
@@ -29,13 +29,19 @@ def tile_conditionalmodel2_kernel(tc, q, k, v, k_past, v_past, base, offs, out):
 
     with (
         tc.tile_pool(name="held", bufs=1) as held,
-        tc.tile_pool(name="weights", bufs=6) as weights,
+        tc.tile_pool(name="weights", bufs=4) as weights,
         tc.tile_pool(name="factors", bufs=2) as factors,
         tc.psum_pool(name="score_banks", bufs=3) as score_banks,
         tc.psum_pool(name="num_banks", bufs=2) as num_banks,
-        tc.psum_pool(name="total_banks", bufs=2) as total_banks,
-        tc.psum_pool(name="spread_banks", bufs=1) as spread_banks,
+        tc.psum_pool(name="total_banks", bufs=1) as total_banks,
+        tc.psum_pool(name="spread_banks", bufs=2) as spread_banks,
     ):
+        zeros = held.tile([128, 512], BF16, name="zeros")
+        nc.gpsimd.memset(zeros[:], 0.0)
+        warm = spread_banks.tile([128, 512], F32, name="warm", tag="spread")
+        for repeat in range(WARM_UP):
+            nc.tensor.matmul(warm[:], zeros[:, 0:128], zeros[:], start=True, stop=True)
+
         keys = [held.tile([FEATURES, TOKENS], BF16, name=f"keys{h}") for h in range(HEADS)]
         queries = [held.tile([FEATURES, NEW], BF16, name=f"queries{h}") for h in range(HEADS)]
         windows = [held.tile([FEATURES, SLOTS], F32, name=f"window{h}") for h in range(HEADS)]
@@ -44,21 +50,15 @@ def tile_conditionalmodel2_kernel(tc, q, k, v, k_past, v_past, base, offs, out):
         head_rows = [slice(h * FEATURES, (h + 1) * FEATURES) for h in range(HEADS)]
         nc.sync.dma_start(keys[0][:, 0:PAST], k_past[head_rows[0], :])
         nc.scalar.dma_start(queries[0][:], q[head_rows[0], :])
-        nc.scalar.dma_start(vals[:, 0 : PAST // 128, :], v_past.rearrange("(b p) c -> p b c", p=128))
         nc.sync.dma_start(keys[0][:, PAST:TOKENS], k[head_rows[0], :])
-        nc.scalar.dma_start(vals[:, PAST // 128 : BLOCKS, :], v.rearrange("(b p) c -> p b c", p=128))
+        nc.sync.dma_start(vals[:, 0 : PAST // 128, :], v_past.rearrange("(b p) c -> p b c", p=128))
+        nc.sync.dma_start(vals[:, PAST // 128 : BLOCKS, :], v.rearrange("(b p) c -> p b c", p=128))
         nc.sync.dma_start(keys[1][:, 0:PAST], k_past[head_rows[1], :])
-        nc.scalar.dma_start(queries[1][:], q[head_rows[1], :])
+        nc.sync.dma_start(queries[1][:], q[head_rows[1], :])
         nc.sync.dma_start(keys[1][:, PAST:TOKENS], k[head_rows[1], :])
         nc.sync.dma_start(offsets[:], offs)
-        nc.sync.dma_start(windows[0][:], base[head_rows[0], :])
-        nc.scalar.dma_start(windows[1][:], base[head_rows[1], :])
-
-        zeros = held.tile([128, 512], BF16, name="zeros")
-        nc.vector.memset(zeros[:], 0.0)
-        warm = spread_banks.tile([128, 512], F32, name="warm", tag="spread")
-        for repeat in range(WARM_UP):
-            nc.tensor.matmul(warm[:], zeros[:, 0:128], zeros[:], start=True, stop=True)
+        for h in range(HEADS):
+            nc.sync.dma_start(windows[h][:], base[head_rows[h], :])
 
         picks = held.tile([128, SUBS, SUBS], BF16, name="picks")
         nc.vector.memset(picks[:], 0.0)
@@ -67,72 +67,47 @@ def tile_conditionalmodel2_kernel(tc, q, k, v, k_past, v_past, base, offs, out):
         identity = held.tile([128, 128], F32, name="identity")
         make_identity(nc, identity[:])
 
-        work = [(h, piece) for h in range(HEADS) for piece in range(PIECES)]
-        nums, totals, r_columns, factor_pairs = {}, {}, {}, {}
-
-        def attend(c, b):
-            h, piece = work[c]
-            first, last = b == 0, b == BLOCKS - 1
-            if first:
-                nums[c] = num_banks.tile([FEATURES, PIECE], F32, name="num")
-                totals[c] = total_banks.tile([128, SUBS], F32, name="totals")
-            scores = score_banks.tile([128, PIECE], F32, name="scores")
-            nc.tensor.matmul(
-                scores[:],
-                keys[h][:, b * 128 : (b + 1) * 128],
-                queries[h][:, piece * PIECE : (piece + 1) * PIECE],
-                start=True,
-                stop=True,
-            )
-            e = weights.tile([128, PIECE], BF16, name="e")
-            nc.scalar.activation(e[:], scores[:], exp, scale=1.0 / math.sqrt(FEATURES))
-            nc.tensor.matmul(nums[c][:], vals[:, b, head_rows[h]], e[:], start=first, stop=last)
-            for s in range(SUBS):
-                nc.tensor.matmul(
-                    totals[c][:],
-                    e[:, s * 128 : (s + 1) * 128],
-                    picks[:, s, :],
-                    start=first and s == 0,
-                    stop=last and s == SUBS - 1,
-                )
-
-        def invert(c):
-            r_columns[c] = factors.tile([128, SUBS], F32, name="r_column")
-            nc.vector.reciprocal(r_columns[c][:], totals[c][:])
-
-        def spread(c):
-            r_rows = spread_banks.tile([FEATURES, PIECE], F32, name="r_rows", tag="spread")
-            for s in range(SUBS):
-                nc.tensor.transpose(
-                    r_rows[:, s * 128 : (s + 1) * 128], r_columns[c][:, s : s + 1].to_broadcast([128, 128]), identity[:]
-                )
-            num_sb = factors.tile([FEATURES, PIECE], F32, name="num_sb")
-            nc.scalar.copy(num_sb[:], nums[c][:])
-            r = factors.tile([FEATURES, PIECE], F32, name="r")
-            nc.scalar.copy(r[:], r_rows[:])
-            factor_pairs[c] = (num_sb, r)
-
-        def place(c):
-            h, piece = work[c]
-            num_sb, r = factor_pairs[c]
-            nc.vector.tensor_tensor(
-                windows[h][:].indirect(offsets[:, piece * (PIECE // 16) : (piece + 1) * (PIECE // 16)]),
-                num_sb[:],
-                r[:],
-                mult,
-            )
-            if piece == PIECES - 1:
-                half = SLOTS // 2
-                nc.sync.dma_start(out[head_rows[h], 0:half], windows[h][:, 0:half])
-                nc.scalar.dma_start(out[head_rows[h], half:SLOTS], windows[h][:, half:SLOTS])
-
-        for c in range(len(work)):
+        for h in range(HEADS):
+            num = num_banks.tile([FEATURES, NEW], F32, name="num")
+            totals = total_banks.tile([128, SUBS], F32, name="totals")
             for b in range(BLOCKS):
-                attend(c, b)
-                if b == 1 and c > 0:
-                    spread(c - 1)
-            invert(c)
-            if c > 0:
-                place(c - 1)
-        spread(len(work) - 1)
-        place(len(work) - 1)
+                first, last = b == 0, b == BLOCKS - 1
+                scores = score_banks.tile([128, NEW], F32, name="scores")
+                nc.tensor.matmul(scores[:], keys[h][:, b * 128 : (b + 1) * 128], queries[h][:], start=True, stop=True)
+                e = weights.tile([128, NEW], BF16, name="e")
+                nc.scalar.activation(e[:], scores[:], exp, scale=1.0 / math.sqrt(FEATURES))
+                nc.tensor.matmul(num[:], vals[:, b, head_rows[h]], e[:], start=first, stop=last)
+                for s in range(SUBS):
+                    nc.tensor.matmul(
+                        totals[:],
+                        e[:, s * 128 : (s + 1) * 128],
+                        picks[:, s, :],
+                        start=first and s == 0,
+                        stop=last and s == SUBS - 1,
+                    )
+            r_column = factors.tile([128, SUBS], F32, name="r_column")
+            nc.vector.reciprocal(r_column[:], totals[:])
+
+            for piece in range(PIECES):
+                columns = slice(piece * PIECE, (piece + 1) * PIECE)
+                r_rows = spread_banks.tile([FEATURES, PIECE], F32, name="r_rows", tag="spread")
+                for i in range(PIECE // 128):
+                    s = piece * (PIECE // 128) + i
+                    nc.tensor.transpose(
+                        r_rows[:, i * 128 : (i + 1) * 128], r_column[:, s : s + 1].to_broadcast([128, 128]), identity[:]
+                    )
+                num_sb = factors.tile([FEATURES, PIECE], F32, name="num_sb")
+                r = factors.tile([FEATURES, PIECE], F32, name="r")
+                if h == HEADS - 1:
+                    nc.scalar.copy(num_sb[:], num[:, columns])
+                    nc.scalar.copy(r[:], r_rows[:])
+                else:
+                    nc.vector.tensor_copy(num_sb[:], num[:, columns])
+                    nc.vector.tensor_copy(r[:], r_rows[:])
+                nc.vector.tensor_tensor(
+                    windows[h][:].indirect(offsets[:, piece * (PIECE // 16) : (piece + 1) * (PIECE // 16)]),
+                    num_sb[:],
+                    r[:],
+                    mult,
+                )
+            nc.sync.dma_start(out[head_rows[h], :], windows[h][:])

@@ -10,10 +10,11 @@ NEW = 512
 SLOTS = 1024
 TOKENS = PAST + NEW
 BLOCKS = TOKENS // 128
-SUBS = NEW // 128
+BANK = 512
 PIECE = 256
-PIECES = NEW // PIECE
 WARM_UP = 3
+
+ITEMS = ((0, 0, 256), (0, 256, 256), (1, 0, 512))
 
 BF16 = mybir.dt.bfloat16
 F32 = mybir.dt.float32
@@ -33,12 +34,12 @@ def tile_conditionalmodel2_kernel(tc, q, k, v, k_past, v_past, base, offs, out):
         tc.tile_pool(name="factors", bufs=2) as factors,
         tc.psum_pool(name="score_banks", bufs=3) as score_banks,
         tc.psum_pool(name="num_banks", bufs=2) as num_banks,
-        tc.psum_pool(name="total_banks", bufs=1) as total_banks,
-        tc.psum_pool(name="spread_banks", bufs=2) as spread_banks,
+        tc.psum_pool(name="total_banks", bufs=2) as total_banks,
+        tc.psum_pool(name="spread_banks", bufs=1) as spread_banks,
     ):
-        zeros = held.tile([128, 512], BF16, name="zeros")
+        zeros = held.tile([128, BANK], BF16, name="zeros")
         nc.gpsimd.memset(zeros[:], 0.0)
-        warm = spread_banks.tile([128, 512], F32, name="warm", tag="spread")
+        warm = spread_banks.tile([128, BANK], F32, name="warm", tag="spread")
         for repeat in range(WARM_UP):
             nc.tensor.matmul(warm[:], zeros[:, 0:128], zeros[:], start=True, stop=True)
 
@@ -53,43 +54,54 @@ def tile_conditionalmodel2_kernel(tc, q, k, v, k_past, v_past, base, offs, out):
         nc.sync.dma_start(keys[0][:, PAST:TOKENS], k[head_rows[0], :])
         nc.sync.dma_start(vals[:, 0 : PAST // 128, :], v_past.rearrange("(b p) c -> p b c", p=128))
         nc.sync.dma_start(vals[:, PAST // 128 : BLOCKS, :], v.rearrange("(b p) c -> p b c", p=128))
+        nc.sync.dma_start(offsets[:], offs)
+        nc.sync.dma_start(windows[0][:], base[head_rows[0], :])
         nc.sync.dma_start(keys[1][:, 0:PAST], k_past[head_rows[1], :])
         nc.sync.dma_start(queries[1][:], q[head_rows[1], :])
         nc.sync.dma_start(keys[1][:, PAST:TOKENS], k[head_rows[1], :])
-        nc.sync.dma_start(offsets[:], offs)
-        for h in range(HEADS):
-            nc.sync.dma_start(windows[h][:], base[head_rows[h], :])
+        nc.sync.dma_start(windows[1][:], base[head_rows[1], :])
 
-        picks = held.tile([128, SUBS, SUBS], BF16, name="picks")
+        most_subs = NEW // 128
+        picks = held.tile([128, most_subs, most_subs], BF16, name="picks")
         nc.vector.memset(picks[:], 0.0)
-        for s in range(SUBS):
+        for s in range(most_subs):
             nc.vector.memset(picks[:, s, s : s + 1], 1.0)
         identity = held.tile([128, 128], F32, name="identity")
         make_identity(nc, identity[:])
 
-        for h in range(HEADS):
-            num = num_banks.tile([FEATURES, NEW], F32, name="num")
-            totals = total_banks.tile([128, SUBS], F32, name="totals")
-            for b in range(BLOCKS):
-                first, last = b == 0, b == BLOCKS - 1
-                scores = score_banks.tile([128, NEW], F32, name="scores")
-                nc.tensor.matmul(scores[:], keys[h][:, b * 128 : (b + 1) * 128], queries[h][:], start=True, stop=True)
-                e = weights.tile([128, NEW], BF16, name="e")
-                nc.scalar.activation(e[:], scores[:], exp, scale=1.0 / math.sqrt(FEATURES))
-                nc.tensor.matmul(num[:], vals[:, b, head_rows[h]], e[:], start=first, stop=last)
-                for s in range(SUBS):
+        for h, start, width in ITEMS:
+            subs = width // 128
+            group = BANK // width
+            num = num_banks.tile([FEATURES, width], F32, name="num")
+            totals = total_banks.tile([128, subs], F32, name="totals")
+            for first_block in range(0, BLOCKS, group):
+                blocks = range(first_block, first_block + group)
+                scores = score_banks.tile([128, group, width], F32, name="scores")
+                for g, b in enumerate(blocks):
                     nc.tensor.matmul(
-                        totals[:],
-                        e[:, s * 128 : (s + 1) * 128],
-                        picks[:, s, :],
-                        start=first and s == 0,
-                        stop=last and s == SUBS - 1,
+                        scores[:, g, :],
+                        keys[h][:, b * 128 : (b + 1) * 128],
+                        queries[h][:, start : start + width],
+                        start=True,
+                        stop=True,
                     )
-            r_column = factors.tile([128, SUBS], F32, name="r_column")
+                e = weights.tile([128, group, width], BF16, name="e")
+                nc.scalar.activation(e[:], scores[:], exp, scale=1.0 / math.sqrt(FEATURES))
+                for g, b in enumerate(blocks):
+                    first, last = b == 0, b == BLOCKS - 1
+                    nc.tensor.matmul(num[:], vals[:, b, head_rows[h]], e[:, g, :], start=first, stop=last)
+                    for s in range(subs):
+                        nc.tensor.matmul(
+                            totals[:],
+                            e[:, g, s * 128 : (s + 1) * 128],
+                            picks[:, s, 0:subs],
+                            start=first and s == 0,
+                            stop=last and s == subs - 1,
+                        )
+            r_column = factors.tile([128, subs], F32, name="r_column")
             nc.vector.reciprocal(r_column[:], totals[:])
 
-            for piece in range(PIECES):
-                columns = slice(piece * PIECE, (piece + 1) * PIECE)
+            for piece in range(width // PIECE):
                 r_rows = spread_banks.tile([FEATURES, PIECE], F32, name="r_rows", tag="spread")
                 for i in range(PIECE // 128):
                     s = piece * (PIECE // 128) + i
@@ -98,16 +110,15 @@ def tile_conditionalmodel2_kernel(tc, q, k, v, k_past, v_past, base, offs, out):
                     )
                 num_sb = factors.tile([FEATURES, PIECE], F32, name="num_sb")
                 r = factors.tile([FEATURES, PIECE], F32, name="r")
-                if h == HEADS - 1:
-                    nc.scalar.copy(num_sb[:], num[:, columns])
+                if (h, start, width) == ITEMS[-1]:
+                    nc.scalar.copy(num_sb[:], num[:, piece * PIECE : (piece + 1) * PIECE])
                     nc.scalar.copy(r[:], r_rows[:])
                 else:
-                    nc.vector.tensor_copy(num_sb[:], num[:, columns])
+                    nc.vector.tensor_copy(num_sb[:], num[:, piece * PIECE : (piece + 1) * PIECE])
                     nc.vector.tensor_copy(r[:], r_rows[:])
+                entry = start + piece * PIECE
                 nc.vector.tensor_tensor(
-                    windows[h][:].indirect(offsets[:, piece * (PIECE // 16) : (piece + 1) * (PIECE // 16)]),
-                    num_sb[:],
-                    r[:],
-                    mult,
+                    windows[h][:].indirect(offsets[:, entry // 16 : (entry + PIECE) // 16]), num_sb[:], r[:], mult
                 )
-            nc.sync.dma_start(out[head_rows[h], :], windows[h][:])
+            if start + width == NEW:
+                nc.sync.dma_start(out[head_rows[h], :], windows[h][:])

@@ -11,10 +11,12 @@ SLOTS = 1024
 TOKENS = PAST + NEW
 BLOCKS = TOKENS // 128
 BANK = 512
-PIECE = 256
+ITEM = 256
+SUBS = ITEM // 128
+PAIR = BANK // ITEM
+PIECE = 128
+AHEAD = 2
 WARM_UP = 3
-
-ITEMS = ((0, 0, 256), (0, 256, 256), (1, 0, 512))
 
 BF16 = mybir.dt.bfloat16
 F32 = mybir.dt.float32
@@ -30,9 +32,9 @@ def tile_conditionalmodel2_kernel(tc, q, k, v, k_past, v_past, base, offs, out):
 
     with (
         tc.tile_pool(name="held", bufs=1) as held,
-        tc.tile_pool(name="weights", bufs=4) as weights,
-        tc.tile_pool(name="factors", bufs=2) as factors,
-        tc.psum_pool(name="score_banks", bufs=3) as score_banks,
+        tc.tile_pool(name="weights", bufs=AHEAD + 2) as weights,
+        tc.tile_pool(name="factors", bufs=3) as factors,
+        tc.psum_pool(name="score_banks", bufs=AHEAD + 1) as score_banks,
         tc.psum_pool(name="num_banks", bufs=2) as num_banks,
         tc.psum_pool(name="total_banks", bufs=2) as total_banks,
         tc.psum_pool(name="spread_banks", bufs=1) as spread_banks,
@@ -61,64 +63,105 @@ def tile_conditionalmodel2_kernel(tc, q, k, v, k_past, v_past, base, offs, out):
         nc.sync.dma_start(keys[1][:, PAST:TOKENS], k[head_rows[1], :])
         nc.sync.dma_start(windows[1][:], base[head_rows[1], :])
 
-        most_subs = NEW // 128
-        picks = held.tile([128, most_subs, most_subs], BF16, name="picks")
+        picks = held.tile([128, SUBS, SUBS], BF16, name="picks")
         nc.vector.memset(picks[:], 0.0)
-        for s in range(most_subs):
+        for s in range(SUBS):
             nc.vector.memset(picks[:, s, s : s + 1], 1.0)
         identity = held.tile([128, 128], F32, name="identity")
         make_identity(nc, identity[:])
 
-        for h, start, width in ITEMS:
-            subs = width // 128
-            group = BANK // width
-            num = num_banks.tile([FEATURES, width], F32, name="num")
-            totals = total_banks.tile([128, subs], F32, name="totals")
-            for first_block in range(0, BLOCKS, group):
-                blocks = range(first_block, first_block + group)
-                scores = score_banks.tile([128, group, width], F32, name="scores")
-                for g, b in enumerate(blocks):
-                    nc.tensor.matmul(
-                        scores[:, g, :],
-                        keys[h][:, b * 128 : (b + 1) * 128],
-                        queries[h][:, start : start + width],
-                        start=True,
-                        stop=True,
-                    )
-                e = weights.tile([128, group, width], BF16, name="e")
-                nc.scalar.activation(e[:], scores[:], exp, scale=1.0 / math.sqrt(FEATURES))
-                for g, b in enumerate(blocks):
-                    first, last = b == 0, b == BLOCKS - 1
-                    nc.tensor.matmul(num[:], vals[:, b, head_rows[h]], e[:, g, :], start=first, stop=last)
-                    for s in range(subs):
-                        nc.tensor.matmul(
-                            totals[:],
-                            e[:, g, s * 128 : (s + 1) * 128],
-                            picks[:, s, 0:subs],
-                            start=first and s == 0,
-                            stop=last and s == subs - 1,
-                        )
-            r_column = factors.tile([128, subs], F32, name="r_column")
-            nc.vector.reciprocal(r_column[:], totals[:])
+        items = [(h, start) for h in range(HEADS) for start in range(0, NEW, ITEM)]
+        steps = [(i, first_block) for i in range(len(items)) for first_block in range(0, BLOCKS, PAIR)]
+        e_of_step = {}
+        num_of_item = {}
+        totals_of_item = {}
+        num_sb_of_item = {}
+        r_column_of_item = {}
+        r_of_item = {}
 
-            for piece in range(width // PIECE):
-                r_rows = spread_banks.tile([FEATURES, PIECE], F32, name="r_rows", tag="spread")
-                for i in range(PIECE // 128):
-                    s = piece * (PIECE // 128) + i
-                    nc.tensor.transpose(
-                        r_rows[:, i * 128 : (i + 1) * 128], r_column[:, s : s + 1].to_broadcast([128, 128]), identity[:]
-                    )
-                num_sb = factors.tile([FEATURES, PIECE], F32, name="num_sb")
-                r = factors.tile([FEATURES, PIECE], F32, name="r")
-                if (h, start, width) == ITEMS[-1]:
-                    nc.scalar.copy(num_sb[:], num[:, piece * PIECE : (piece + 1) * PIECE])
-                    nc.scalar.copy(r[:], r_rows[:])
-                else:
-                    nc.vector.tensor_copy(num_sb[:], num[:, piece * PIECE : (piece + 1) * PIECE])
-                    nc.vector.tensor_copy(r[:], r_rows[:])
-                entry = start + piece * PIECE
-                nc.vector.tensor_tensor(
-                    windows[h][:].indirect(offsets[:, entry // 16 : (entry + PIECE) // 16]), num_sb[:], r[:], mult
+        def score_and_exp(t):
+            i, first_block = steps[t]
+            h, start = items[i]
+            scores = score_banks.tile([128, PAIR, ITEM], F32, name="scores")
+            for g in range(PAIR):
+                b = first_block + g
+                nc.tensor.matmul(
+                    scores[:, g, :],
+                    keys[h][:, b * 128 : (b + 1) * 128],
+                    queries[h][:, start : start + ITEM],
+                    start=True,
+                    stop=True,
                 )
-            if start + width == NEW:
+            e = weights.tile([128, PAIR, ITEM], BF16, name="e")
+            nc.scalar.activation(e[:], scores[:], exp, scale=1.0 / math.sqrt(FEATURES))
+            e_of_step[t] = e
+
+        def accumulate(t):
+            i, first_block = steps[t]
+            h, start = items[i]
+            if first_block == 0:
+                num_of_item[i] = num_banks.tile([FEATURES, ITEM], F32, name="num")
+                totals_of_item[i] = total_banks.tile([128, SUBS], F32, name="totals")
+            e = e_of_step[t]
+            for g in range(PAIR):
+                b = first_block + g
+                first, last = b == 0, b == BLOCKS - 1
+                nc.tensor.matmul(num_of_item[i][:], vals[:, b, head_rows[h]], e[:, g, :], start=first, stop=last)
+                for s in range(SUBS):
+                    nc.tensor.matmul(
+                        totals_of_item[i][:],
+                        e[:, g, s * 128 : (s + 1) * 128],
+                        picks[:, s, :],
+                        start=first and s == 0,
+                        stop=last and s == SUBS - 1,
+                    )
+
+        def invert(i):
+            num_sb = factors.tile([FEATURES, ITEM], F32, name="num_sb")
+            nc.scalar.copy(num_sb[:], num_of_item[i][:])
+            num_sb_of_item[i] = num_sb
+            r_column = factors.tile([128, SUBS], F32, name="r_column")
+            nc.vector.reciprocal(r_column[:], totals_of_item[i][:])
+            r_column_of_item[i] = r_column
+
+        def spread(i):
+            r_rows = spread_banks.tile([FEATURES, ITEM], F32, name="r_rows", tag="spread")
+            for s in range(SUBS):
+                nc.tensor.transpose(
+                    r_rows[:, s * 128 : (s + 1) * 128],
+                    r_column_of_item[i][:, s : s + 1].to_broadcast([128, 128]),
+                    identity[:],
+                )
+            r = factors.tile([FEATURES, ITEM], F32, name="r")
+            nc.vector.tensor_copy(r[:], r_rows[:])
+            r_of_item[i] = r
+
+        def place(i, piece):
+            h, start = items[i]
+            columns = slice(piece * PIECE, (piece + 1) * PIECE)
+            entry = start + piece * PIECE
+            nc.vector.tensor_tensor(
+                windows[h][:].indirect(offsets[:, entry // 16 : (entry + PIECE) // 16]),
+                num_sb_of_item[i][:, columns],
+                r_of_item[i][:, columns],
+                mult,
+            )
+            if entry + PIECE == NEW:
                 nc.sync.dma_start(out[head_rows[h], :], windows[h][:])
+
+        for t in range(len(steps) + AHEAD):
+            if t < len(steps):
+                score_and_exp(t)
+            if t < AHEAD:
+                continue
+            i, first_block = steps[t - AHEAD]
+            accumulate(t - AHEAD)
+            if first_block == 0 and i > 0:
+                spread(i - 1)
+                for piece in range(ITEM // PIECE):
+                    place(i - 1, piece)
+            if first_block == BLOCKS - PAIR:
+                invert(i)
+        spread(len(items) - 1)
+        for piece in range(ITEM // PIECE):
+            place(len(items) - 1, piece)

@@ -14,7 +14,7 @@ BANK = 512
 ITEM = 256
 SUBS = ITEM // 128
 PAIR = BANK // ITEM
-PIECE = 128
+PIECE = 256
 AHEAD = 2
 WARM_UP = 3
 
@@ -105,24 +105,27 @@ def tile_conditionalmodel2_kernel(tc, q, k, v, k_past, v_past, base, offs, out):
             e = e_of_step[t]
             for g in range(PAIR):
                 b = first_block + g
-                first, last = b == 0, b == BLOCKS - 1
-                nc.tensor.matmul(num_of_item[i][:], vals[:, b, head_rows[h]], e[:, g, :], start=first, stop=last)
                 for s in range(SUBS):
                     nc.tensor.matmul(
                         totals_of_item[i][:],
                         e[:, g, s * 128 : (s + 1) * 128],
                         picks[:, s, :],
-                        start=first and s == 0,
-                        stop=last and s == SUBS - 1,
+                        start=b == 0 and s == 0,
+                        stop=b == BLOCKS - 1 and s == SUBS - 1,
                     )
+            for g in range(PAIR):
+                b = first_block + g
+                nc.tensor.matmul(
+                    num_of_item[i][:], vals[:, b, head_rows[h]], e[:, g, :], start=b == 0, stop=b == BLOCKS - 1
+                )
 
         def invert(i):
-            num_sb = factors.tile([FEATURES, ITEM], F32, name="num_sb")
-            nc.scalar.copy(num_sb[:], num_of_item[i][:])
-            num_sb_of_item[i] = num_sb
             r_column = factors.tile([128, SUBS], F32, name="r_column")
             nc.vector.reciprocal(r_column[:], totals_of_item[i][:])
             r_column_of_item[i] = r_column
+            num_sb = factors.tile([FEATURES, ITEM], F32, name="num_sb")
+            nc.scalar.copy(num_sb[:], num_of_item[i][:])
+            num_sb_of_item[i] = num_sb
 
         def spread(i):
             r_rows = spread_banks.tile([FEATURES, ITEM], F32, name="r_rows", tag="spread")
@@ -133,7 +136,9 @@ def tile_conditionalmodel2_kernel(tc, q, k, v, k_past, v_past, base, offs, out):
                     identity[:],
                 )
             r = factors.tile([FEATURES, ITEM], F32, name="r")
-            nc.vector.tensor_copy(r[:], r_rows[:])
+            for piece in range(ITEM // PIECE):
+                columns = slice(piece * PIECE, (piece + 1) * PIECE)
+                nc.scalar.copy(r[:, columns], r_rows[:, columns])
             r_of_item[i] = r
 
         def place(i, piece):

@@ -54,13 +54,13 @@ def tile_conditionalmodel2_kernel(tc, q, k, v, k_past, v_past, base, offs, out):
         nc.sync.dma_start(keys[0][:, 0:PAST], k_past[head_rows[0], :])
         nc.scalar.dma_start(queries[0][:], q[head_rows[0], :])
         nc.sync.dma_start(keys[0][:, PAST:TOKENS], k[head_rows[0], :])
+        nc.scalar.dma_start(queries[1][:], q[head_rows[1], :])
         nc.sync.dma_start(vals[:, 0 : PAST // 128, :], v_past.rearrange("(b p) c -> p b c", p=128))
+        nc.sync.dma_start(keys[1][:, 0:PAST], k_past[head_rows[1], :])
         nc.sync.dma_start(vals[:, PAST // 128 : BLOCKS, :], v.rearrange("(b p) c -> p b c", p=128))
+        nc.sync.dma_start(keys[1][:, PAST:TOKENS], k[head_rows[1], :])
         nc.sync.dma_start(offsets[:], offs)
         nc.sync.dma_start(windows[0][:], base[head_rows[0], :])
-        nc.sync.dma_start(keys[1][:, 0:PAST], k_past[head_rows[1], :])
-        nc.sync.dma_start(queries[1][:], q[head_rows[1], :])
-        nc.sync.dma_start(keys[1][:, PAST:TOKENS], k[head_rows[1], :])
         nc.sync.dma_start(windows[1][:], base[head_rows[1], :])
 
         picks = held.tile([128, SUBS, SUBS], BF16, name="picks")
@@ -70,7 +70,7 @@ def tile_conditionalmodel2_kernel(tc, q, k, v, k_past, v_past, base, offs, out):
         identity = held.tile([128, 128], F32, name="identity")
         make_identity(nc, identity[:])
 
-        items = [(h, start) for h in range(HEADS) for start in range(0, NEW, ITEM)]
+        items = [(h, start) for start in range(0, NEW, ITEM) for h in range(HEADS)]
         steps = [(i, first_block) for i in range(len(items)) for first_block in range(0, BLOCKS, PAIR)]
         e_of_step = {}
         num_of_item = {}

@@ -52,15 +52,17 @@ def tile_conditionalmodel2_kernel(tc, q, k, v, k_past, v_past, base, offs, out):
         offsets = held.tile([128, NEW // 16], U16, name="offsets")
         head_rows = [slice(h * FEATURES, (h + 1) * FEATURES) for h in range(HEADS)]
         nc.sync.dma_start(keys[0][:, 0:PAST], k_past[head_rows[0], :])
-        nc.scalar.dma_start(queries[0][:], q[head_rows[0], :])
+        nc.scalar.dma_start(queries[0][:, 0:ITEM], q[head_rows[0], 0:ITEM])
         nc.sync.dma_start(keys[0][:, PAST:TOKENS], k[head_rows[0], :])
-        nc.scalar.dma_start(queries[1][:], q[head_rows[1], :])
+        nc.scalar.dma_start(queries[1][:, 0:ITEM], q[head_rows[1], 0:ITEM])
         nc.sync.dma_start(vals[:, 0 : PAST // 128, :], v_past.rearrange("(b p) c -> p b c", p=128))
         nc.sync.dma_start(keys[1][:, 0:PAST], k_past[head_rows[1], :])
         nc.sync.dma_start(vals[:, PAST // 128 : BLOCKS, :], v.rearrange("(b p) c -> p b c", p=128))
         nc.sync.dma_start(keys[1][:, PAST:TOKENS], k[head_rows[1], :])
         nc.sync.dma_start(offsets[:], offs)
         nc.sync.dma_start(windows[0][:], base[head_rows[0], :])
+        nc.sync.dma_start(queries[0][:, ITEM:NEW], q[head_rows[0], ITEM:NEW])
+        nc.sync.dma_start(queries[1][:, ITEM:NEW], q[head_rows[1], ITEM:NEW])
         nc.sync.dma_start(windows[1][:], base[head_rows[1], :])
 
         picks = held.tile([128, SUBS, SUBS], BF16, name="picks")

@@ -16,7 +16,7 @@ SUBS = ITEM // 128
 PAIR = BANK // ITEM
 PIECE = 256
 AHEAD = 2
-WARM_UP = 3
+WARM_UP = 2
 
 BF16 = mybir.dt.bfloat16
 F32 = mybir.dt.float32

@@ -55,9 +55,9 @@ def tile_conditionalmodel2_kernel(tc, q, k, v, k_past, v_past, base, offs, out):
         nc.scalar.dma_start(queries[0][:, 0:ITEM], q[head_rows[0], 0:ITEM])
         nc.sync.dma_start(keys[0][:, PAST:TOKENS], k[head_rows[0], :])
         nc.scalar.dma_start(queries[1][:, 0:ITEM], q[head_rows[1], 0:ITEM])
-        nc.sync.dma_start(vals[:, 0 : PAST // 128, :], v_past.rearrange("(b p) c -> p b c", p=128))
+        nc.sync.dma_start(vals[:, 0 : PAST // 128, :], v_past.rearrange("(p b) c -> p b c", p=128))
         nc.sync.dma_start(keys[1][:, 0:PAST], k_past[head_rows[1], :])
-        nc.sync.dma_start(vals[:, PAST // 128 : BLOCKS, :], v.rearrange("(b p) c -> p b c", p=128))
+        nc.sync.dma_start(vals[:, PAST // 128 : BLOCKS, :], v.rearrange("(p b) c -> p b c", p=128))
         nc.sync.dma_start(keys[1][:, PAST:TOKENS], k[head_rows[1], :])
         nc.sync.dma_start(offsets[:], offs)
         nc.sync.dma_start(windows[0][:], base[head_rows[0], :])
@@ -81,6 +81,12 @@ def tile_conditionalmodel2_kernel(tc, q, k, v, k_past, v_past, base, offs, out):
         r_column_of_item = {}
         r_of_item = {}
 
+        def block_of_keys(h, b):
+            past_blocks = PAST // 128
+            if b < past_blocks:
+                return keys[h][:, b:PAST:past_blocks]
+            return keys[h][:, PAST + b - past_blocks : TOKENS : NEW // 128]
+
         def score_and_exp(t):
             i, first_block = steps[t]
             h, start = items[i]
@@ -89,7 +95,7 @@ def tile_conditionalmodel2_kernel(tc, q, k, v, k_past, v_past, base, offs, out):
                 b = first_block + g
                 nc.tensor.matmul(
                     scores[:, g, :],
-                    keys[h][:, b * 128 : (b + 1) * 128],
+                    block_of_keys(h, b),
                     queries[h][:, start : start + ITEM],
                     start=True,
                     stop=True,

@@ -1,7 +1,6 @@
 import math
 
 import concourse.mybir as mybir
-from concourse.masks import make_identity
 
 HEADS = 2
 FEATURES = 128
@@ -16,6 +15,8 @@ SUBS = ITEM // 128
 PAIR = BANK // ITEM
 PIECE = 256
 AHEAD = 2
+LAG = 2
+QUARTER = 32
 WARM_UP = 2
 
 BF16 = mybir.dt.bfloat16
@@ -69,8 +70,19 @@ def tile_conditionalmodel2_kernel(tc, q, k, v, k_past, v_past, base, offs, out):
         nc.vector.memset(picks[:], 0.0)
         for s in range(SUBS):
             nc.vector.memset(picks[:, s, s : s + 1], 1.0)
+        steps_of_one = held.tile([128, QUARTER], F32, name="steps_of_one")
+        nc.vector.memset(steps_of_one[:], 1.0)
+        column = held.tile([128, QUARTER], F32, name="column", align_bytes=64)
+        nc.vector.tensor_tensor_scan(column[:], steps_of_one[:], steps_of_one[:], 0.0, mult, mybir.AluOpType.add)
+        row = held.tile([128, QUARTER], F32, name="row", align_bytes=64)
+        nc.vector.transpose(row[:], column[:])
         identity = held.tile([128, 128], F32, name="identity")
-        make_identity(nc, identity[:])
+        nc.vector.memset(identity[:], 0.0)
+        for start in range(0, 128, QUARTER):
+            quarter = slice(start, start + QUARTER)
+            nc.vector.tensor_tensor(
+                identity[quarter, quarter], column[quarter, :], row[quarter, :], mybir.AluOpType.is_equal
+            )
 
         items = [(h, start) for start in range(0, NEW, ITEM) for h in range(HEADS)]
         steps = [(i, first_block) for i in range(len(items)) for first_block in range(0, BLOCKS, PAIR)]
@@ -162,19 +174,18 @@ def tile_conditionalmodel2_kernel(tc, q, k, v, k_past, v_past, base, offs, out):
             if entry + PIECE == NEW:
                 nc.sync.dma_start(out[head_rows[h], :], windows[h][:])
 
-        for t in range(len(steps) + AHEAD):
+        last_block = BLOCKS - PAIR
+        for t in range(len(steps) + AHEAD + LAG):
             if t < len(steps):
                 score_and_exp(t)
-            if t < AHEAD:
-                continue
-            i, first_block = steps[t - AHEAD]
-            accumulate(t - AHEAD)
-            if first_block == 0 and i > 0:
-                spread(i - 1)
-                for piece in range(ITEM // PIECE):
-                    place(i - 1, piece)
-            if first_block == BLOCKS - PAIR:
-                invert(i)
-        spread(len(items) - 1)
-        for piece in range(ITEM // PIECE):
-            place(len(items) - 1, piece)
+            if AHEAD <= t < len(steps) + AHEAD:
+                i, first_block = steps[t - AHEAD]
+                accumulate(t - AHEAD)
+                if first_block == last_block:
+                    invert(i)
+            if t >= AHEAD + LAG:
+                i, first_block = steps[t - AHEAD - LAG]
+                if first_block == last_block:
+                    spread(i)
+                    for piece in range(ITEM // PIECE):
+                        place(i, piece)

@@ -139,12 +139,18 @@ def tile_conditionalmodel2_kernel(tc, q, k, v, k_past, v_past, base, offs, out):
                     num_of_item[i][:], vals[:, b, head_rows[h]], e[:, g, :], start=b == 0, stop=b == BLOCKS - 1
                 )
 
+        def copy_from_psum(i, to, bank):
+            if i == 0:
+                nc.vector.tensor_copy(to, bank)
+            else:
+                nc.scalar.copy(to, bank)
+
         def invert(i):
             r_column = factors.tile([128, SUBS], F32, name="r_column")
             nc.vector.reciprocal(r_column[:], totals_of_item[i][:])
             r_column_of_item[i] = r_column
             num_sb = factors.tile([FEATURES, ITEM], F32, name="num_sb")
-            nc.scalar.copy(num_sb[:], num_of_item[i][:])
+            copy_from_psum(i, num_sb[:], num_of_item[i][:])
             num_sb_of_item[i] = num_sb
 
         def spread(i):
@@ -158,7 +164,7 @@ def tile_conditionalmodel2_kernel(tc, q, k, v, k_past, v_past, base, offs, out):
             r = factors.tile([FEATURES, ITEM], F32, name="r")
             for piece in range(ITEM // PIECE):
                 columns = slice(piece * PIECE, (piece + 1) * PIECE)
-                nc.scalar.copy(r[:, columns], r_rows[:, columns])
+                copy_from_psum(i, r[:, columns], r_rows[:, columns])
             r_of_item[i] = r
 
         def place(i, piece):
@@ -175,6 +181,12 @@ def tile_conditionalmodel2_kernel(tc, q, k, v, k_past, v_past, base, offs, out):
                 nc.sync.dma_start(out[head_rows[h], :], windows[h][:])
 
         last_block = BLOCKS - PAIR
+
+        def spread_and_place(i):
+            spread(i)
+            for piece in range(ITEM // PIECE):
+                place(i, piece)
+
         for t in range(len(steps) + AHEAD + LAG):
             if t < len(steps):
                 score_and_exp(t)
@@ -183,9 +195,9 @@ def tile_conditionalmodel2_kernel(tc, q, k, v, k_past, v_past, base, offs, out):
                 accumulate(t - AHEAD)
                 if first_block == last_block:
                     invert(i)
+                    if i == 0:
+                        spread_and_place(i)
             if t >= AHEAD + LAG:
                 i, first_block = steps[t - AHEAD - LAG]
-                if first_block == last_block:
-                    spread(i)
-                    for piece in range(ITEM // PIECE):
-                        place(i, piece)
+                if first_block == last_block and i > 0:
+                    spread_and_place(i)

@@ -140,7 +140,7 @@ def tile_conditionalmodel2_kernel(tc, q, k, v, k_past, v_past, base, offs, out):
                 )
 
         def copy_from_psum(i, to, bank):
-            if i == 0:
+            if i < HEADS:
                 nc.vector.tensor_copy(to, bank)
             else:
                 nc.scalar.copy(to, bank)

@@ -61,9 +61,9 @@ def tile_conditionalmodel2_kernel(tc, q, k, v, k_past, v_past, base, offs, out):
         nc.sync.dma_start(vals[:, PAST // 128 : BLOCKS, :], v.rearrange("(p b) c -> p b c", p=128))
         nc.sync.dma_start(keys[1][:, PAST:TOKENS], k[head_rows[1], :])
         nc.sync.dma_start(offsets[:], offs)
-        nc.sync.dma_start(windows[0][:], base[head_rows[0], :])
         nc.sync.dma_start(queries[0][:, ITEM:NEW], q[head_rows[0], ITEM:NEW])
         nc.sync.dma_start(queries[1][:, ITEM:NEW], q[head_rows[1], ITEM:NEW])
+        nc.sync.dma_start(windows[0][:], base[head_rows[0], :])
         nc.sync.dma_start(windows[1][:], base[head_rows[1], :])
 
         picks = held.tile([128, SUBS, SUBS], BF16, name="picks")

import math

import concourse.mybir as mybir

HEADS = 2
FEATURES = 128
PAST = 256
NEW = 512
SLOTS = 1024
TOKENS = PAST + NEW
BLOCKS = TOKENS // 128
BANK = 512
ITEM = 256
SUBS = ITEM // 128
PAIR = BANK // ITEM
PIECE = 256
AHEAD = 2
LAG = 2
QUARTER = 32
WARM_UP = 2

BF16 = mybir.dt.bfloat16
F32 = mybir.dt.float32
U16 = mybir.dt.uint16

FLOPS = 2 * 2 * HEADS * FEATURES * TOKENS * NEW


def tile_conditionalmodel2_kernel(tc, q, k, v, k_past, v_past, base, offs, out):
    nc = tc.nc
    exp = mybir.ActivationFunctionType.Exp
    mult = mybir.AluOpType.mult

    with (
        tc.tile_pool(name="held", bufs=1) as held,
        tc.tile_pool(name="weights", bufs=AHEAD + 2) as weights,
        tc.tile_pool(name="factors", bufs=3) as factors,
        tc.psum_pool(name="score_banks", bufs=AHEAD + 1) as score_banks,
        tc.psum_pool(name="num_banks", bufs=2) as num_banks,
        tc.psum_pool(name="total_banks", bufs=2) as total_banks,
        tc.psum_pool(name="spread_banks", bufs=1) as spread_banks,
    ):
        zeros = held.tile([128, BANK], BF16, name="zeros")
        nc.gpsimd.memset(zeros[:], 0.0)
        warm = spread_banks.tile([128, BANK], F32, name="warm", tag="spread")
        for repeat in range(WARM_UP):
            nc.tensor.matmul(warm[:], zeros[:, 0:128], zeros[:], start=True, stop=True)

        keys = [held.tile([FEATURES, TOKENS], BF16, name=f"keys{h}") for h in range(HEADS)]
        queries = [held.tile([FEATURES, NEW], BF16, name=f"queries{h}") for h in range(HEADS)]
        windows = [held.tile([FEATURES, SLOTS], F32, name=f"window{h}") for h in range(HEADS)]
        vals = held.tile([128, BLOCKS, HEADS * FEATURES], BF16, name="vals")
        offsets = held.tile([128, NEW // 16], U16, name="offsets")
        head_rows = [slice(h * FEATURES, (h + 1) * FEATURES) for h in range(HEADS)]
        nc.sync.dma_start(keys[0][:, 0:PAST], k_past[head_rows[0], :])
        nc.scalar.dma_start(queries[0][:, 0:ITEM], q[head_rows[0], 0:ITEM])
        nc.sync.dma_start(keys[0][:, PAST:TOKENS], k[head_rows[0], :])
        nc.scalar.dma_start(queries[1][:, 0:ITEM], q[head_rows[1], 0:ITEM])
        nc.sync.dma_start(vals[:, 0 : PAST // 128, :], v_past.rearrange("(p b) c -> p b c", p=128))
        nc.sync.dma_start(keys[1][:, 0:PAST], k_past[head_rows[1], :])
        nc.sync.dma_start(vals[:, PAST // 128 : BLOCKS, :], v.rearrange("(p b) c -> p b c", p=128))
        nc.sync.dma_start(keys[1][:, PAST:TOKENS], k[head_rows[1], :])
        nc.sync.dma_start(offsets[:], offs)
        nc.sync.dma_start(queries[0][:, ITEM:NEW], q[head_rows[0], ITEM:NEW])
        nc.sync.dma_start(queries[1][:, ITEM:NEW], q[head_rows[1], ITEM:NEW])
        nc.sync.dma_start(windows[0][:], base[head_rows[0], :])
        nc.sync.dma_start(windows[1][:], base[head_rows[1], :])

        picks = held.tile([128, SUBS, SUBS], BF16, name="picks")
        nc.vector.memset(picks[:], 0.0)
        for s in range(SUBS):
            nc.vector.memset(picks[:, s, s : s + 1], 1.0)
        steps_of_one = held.tile([128, QUARTER], F32, name="steps_of_one")
        nc.vector.memset(steps_of_one[:], 1.0)
        column = held.tile([128, QUARTER], F32, name="column", align_bytes=64)
        nc.vector.tensor_tensor_scan(column[:], steps_of_one[:], steps_of_one[:], 0.0, mult, mybir.AluOpType.add)
        row = held.tile([128, QUARTER], F32, name="row", align_bytes=64)
        nc.vector.transpose(row[:], column[:])
        identity = held.tile([128, 128], F32, name="identity")
        nc.vector.memset(identity[:], 0.0)
        for start in range(0, 128, QUARTER):
            quarter = slice(start, start + QUARTER)
            nc.vector.tensor_tensor(
                identity[quarter, quarter], column[quarter, :], row[quarter, :], mybir.AluOpType.is_equal
            )

        items = [(h, start) for start in range(0, NEW, ITEM) for h in range(HEADS)]
        steps = [(i, first_block) for i in range(len(items)) for first_block in range(0, BLOCKS, PAIR)]
        e_of_step = {}
        num_of_item = {}
        totals_of_item = {}
        num_sb_of_item = {}
        r_column_of_item = {}
        r_of_item = {}

        def block_of_keys(h, b):
            past_blocks = PAST // 128
            if b < past_blocks:
                return keys[h][:, b:PAST:past_blocks]
            return keys[h][:, PAST + b - past_blocks : TOKENS : NEW // 128]

        def score_and_exp(t):
            i, first_block = steps[t]
            h, start = items[i]
            scores = score_banks.tile([128, PAIR, ITEM], F32, name="scores")
            for g in range(PAIR):
                b = first_block + g
                nc.tensor.matmul(
                    scores[:, g, :],
                    block_of_keys(h, b),
                    queries[h][:, start : start + ITEM],
                    start=True,
                    stop=True,
                )
            e = weights.tile([128, PAIR, ITEM], BF16, name="e")
            nc.scalar.activation(e[:], scores[:], exp, scale=1.0 / math.sqrt(FEATURES))
            e_of_step[t] = e

        def accumulate(t):
            i, first_block = steps[t]
            h, start = items[i]
            if first_block == 0:
                num_of_item[i] = num_banks.tile([FEATURES, ITEM], F32, name="num")
                totals_of_item[i] = total_banks.tile([128, SUBS], F32, name="totals")
            e = e_of_step[t]
            for g in range(PAIR):
                b = first_block + g
                for s in range(SUBS):
                    nc.tensor.matmul(
                        totals_of_item[i][:],
                        e[:, g, s * 128 : (s + 1) * 128],
                        picks[:, s, :],
                        start=b == 0 and s == 0,
                        stop=b == BLOCKS - 1 and s == SUBS - 1,
                    )
            for g in range(PAIR):
                b = first_block + g
                nc.tensor.matmul(
                    num_of_item[i][:], vals[:, b, head_rows[h]], e[:, g, :], start=b == 0, stop=b == BLOCKS - 1
                )

        def copy_from_psum(i, to, bank):
            if i < HEADS:
                nc.vector.tensor_copy(to, bank)
            else:
                nc.scalar.copy(to, bank)

        def invert(i):
            r_column = factors.tile([128, SUBS], F32, name="r_column")
            nc.vector.reciprocal(r_column[:], totals_of_item[i][:])
            r_column_of_item[i] = r_column
            num_sb = factors.tile([FEATURES, ITEM], F32, name="num_sb")
            copy_from_psum(i, num_sb[:], num_of_item[i][:])
            num_sb_of_item[i] = num_sb

        def spread(i):
            r_rows = spread_banks.tile([FEATURES, ITEM], F32, name="r_rows", tag="spread")
            for s in range(SUBS):
                nc.tensor.transpose(
                    r_rows[:, s * 128 : (s + 1) * 128],
                    r_column_of_item[i][:, s : s + 1].to_broadcast([128, 128]),
                    identity[:],
                )
            r = factors.tile([FEATURES, ITEM], F32, name="r")
            for piece in range(ITEM // PIECE):
                columns = slice(piece * PIECE, (piece + 1) * PIECE)
                copy_from_psum(i, r[:, columns], r_rows[:, columns])
            r_of_item[i] = r

        def place(i, piece):
            h, start = items[i]
            columns = slice(piece * PIECE, (piece + 1) * PIECE)
            entry = start + piece * PIECE
            nc.vector.tensor_tensor(
                windows[h][:].indirect(offsets[:, entry // 16 : (entry + PIECE) // 16]),
                num_sb_of_item[i][:, columns],
                r_of_item[i][:, columns],
                mult,
            )
            if entry + PIECE == NEW:
                nc.sync.dma_start(out[head_rows[h], :], windows[h][:])

        last_block = BLOCKS - PAIR

        def spread_and_place(i):
            spread(i)
            for piece in range(ITEM // PIECE):
                place(i, piece)

        for t in range(len(steps) + AHEAD + LAG):
            if t < len(steps):
                score_and_exp(t)
            if AHEAD <= t < len(steps) + AHEAD:
                i, first_block = steps[t - AHEAD]
                accumulate(t - AHEAD)
                if first_block == last_block:
                    invert(i)
                    if i == 0:
                        spread_and_place(i)
            if t >= AHEAD + LAG:
                i, first_block = steps[t - AHEAD - LAG]
                if first_block == last_block and i > 0:
                    spread_and_place(i)
